import numpy as np
import ml_dtypes


def mxq(x, axis, fmt="e4m3"):
    dtype, down = {"e4m3": (ml_dtypes.float8_e4m3fn, 7), "e5m2": (ml_dtypes.float8_e5m2, 14)}[fmt]
    v = np.moveaxis(np.asarray(x, np.float32).astype(ml_dtypes.bfloat16).astype(np.float64), axis, -1)
    blocks = v.reshape(v.shape[:-1] + (-1, 32))
    amax = np.abs(blocks).max(-1, keepdims=True)
    byte = np.maximum(np.where(amax > 0, np.frexp(amax)[1] - 1 + 127, 0) - down, 1)
    scale = np.exp2(byte - 127.0)
    codes = (blocks / scale).astype(np.float32).astype(dtype).astype(np.float64)
    return np.moveaxis((codes * scale).reshape(v.shape), -1, axis)


WIDE = False


def mx_kscale(k):
    if not WIDE:
        return np.ones(k)
    levels = np.array([10, -10, 5, -5, 0])
    a = np.random.permutation(np.resize(levels, k // 512 * 4)).reshape(k // 512, 4)
    idx = np.arange(k)
    return np.exp2(a[idx // 512, idx % 128 // 32])


BF16 = ml_dtypes.bfloat16


def bf(x):
    return np.asarray(x, np.float32).astype(BF16)


def f64(x):
    return np.asarray(x).astype(np.float64)


B, I, H, S = 512, 512, 1024, 4096
LAM_DIRECT = 1.0
LAM_SPARSE = 1.0
SIG = 1.0
EPS = 0.0001
G = 1.5


def setup_inputs():
    si, sh, ss = mx_kscale(I), mx_kscale(H), mx_kscale(S)
    z = np.random.standard_normal((B, S)) * G * np.sqrt(2.0)
    e = np.exp(z - z.max(axis=1, keepdims=True))
    sy = e / e.sum(axis=1, keepdims=True)
    return {"x": bf(np.random.standard_normal((B, I)) * si),
            "hx": bf(np.random.standard_normal((B, H)) * sh),
            "sy": bf(sy * ss),
            "internal": bf(np.random.standard_normal((B, H))),
            "W_ih": bf(np.random.standard_normal((H, I)) * 0.7 / np.sqrt(I) / si),
            "W_hh": bf(np.random.standard_normal((H, H)) * 0.7 / np.sqrt(H) / sh),
            "W_sh": bf(np.random.standard_normal((H, S)) * 3.0 / ss),
            "mu": bf(np.random.standard_normal(H) * 0.3)}


def reference(x, hx, sy, internal, W_ih, W_hh, W_sh, mu):
    direct = mxq(f64(x), 1, "e4m3") @ mxq(f64(W_ih).T, 0, "e4m3")
    recur = mxq(f64(hx), 1, "e4m3") @ mxq(f64(W_hh).T, 0, "e4m3")
    sparse = mxq(f64(sy), 1, "e4m3") @ mxq(f64(W_sh).T, 0, "e4m3")
    pre = LAM_DIRECT * direct + recur + LAM_SPARSE * sparse
    m = pre.mean(-1, keepdims=True)
    sd = np.sqrt(((pre - m) ** 2).mean(-1, keepdims=True)) + EPS
    ln = (pre - m) / sd * SIG + f64(mu)
    return np.maximum(ln + f64(internal), 0.0)

@@ -1,0 +1,199 @@
+from contextlib import ExitStack
+
+import concourse.mybir as mybir
+from concourse.masks import make_identity
+
+F32 = mybir.dt.float32
+BF16 = mybir.dt.bfloat16
+U32 = mybir.dt.uint32
+U8 = mybir.dt.uint8
+FP8X4 = mybir.dt.float8_e4m3fn_x4
+ALU = mybir.AluOpType
+ACT = mybir.ActivationFunctionType
+
+P = 128
+PACK = 4
+K_PASS = P * PACK
+PASS_WORDS = K_PASS // 2
+B, H = 512, 1024
+B_TILES = B // P
+H_HALF = 512
+SLAB_ROWS = 512
+ROW_TILES = SLAB_ROWS // P
+K_TOTAL = 512 + 1024 + 4096
+PASSES = K_TOTAL // K_PASS
+K_CHUNK = 2 * K_PASS
+RAW_BUFS = 8
+EPS = 0.0001
+
+FLOPS = 2 * B * H * K_TOTAL
+
+
+def tile_sparsegatedrnncell_pb_kernel(tc, x, hx, sy, internal, W_ih, W_hh, W_sh, mu, out):
+    nc = tc.nc
+    with ExitStack() as ctx:
+        const = ctx.enter_context(tc.tile_pool(name="const", bufs=1))
+        keep = ctx.enter_context(tc.tile_pool(name="keep", bufs=1))
+        raw_pool = ctx.enter_context(tc.tile_pool(name="raw_pool", bufs=RAW_BUFS))
+        stage = ctx.enter_context(tc.tile_pool(name="stage", bufs=4))
+        banks = ctx.enter_context(tc.psum_pool(name="banks", bufs=4))
+        sums = ctx.enter_context(tc.psum_pool(name="sums", bufs=4))
+        ctx.enter_context(tc.manual_schedule())
+
+        chunks = []
+        where_is = []
+        for act, weight in ((x, W_ih), (hx, W_hh), (sy, W_sh)):
+            for k0 in range(0, act.shape[1], K_CHUNK):
+                width = min(K_CHUNK, act.shape[1] - k0)
+                for local in range(width // K_PASS):
+                    where_is.append((len(chunks), local, width, local == width // K_PASS - 1))
+                chunks.append((act, weight, k0, width))
+        loads = []
+        for n, (act, weight, k0, width) in enumerate(chunks):
+            loads.append((("act", n), act, 0, k0, width))
+            loads.append((("w", 0, n), weight, 0, k0, width))
+        for n, (act, weight, k0, width) in enumerate(chunks):
+            loads.append((("w", 1, n), weight, H_HALF, k0, width))
+        raw = {}
+
+        def issue_loads(count):
+            for key, source, row0, k0, width in loads[len(raw) : len(raw) + count]:
+                rows = raw_pool.tile([P, ROW_TILES * K_CHUNK], BF16, name="rows", tag="rows")
+                nc.sync.dma_start(
+                    out=rows[:, 0 : ROW_TILES * width].rearrange("p (j k) -> p j k", j=ROW_TILES),
+                    in_=source[row0 : row0 + SLAB_ROWS, k0 : k0 + width].rearrange("(j p) k -> p j k", p=P),
+                )
+                raw[key] = rows
+
+        mu_rows = const.tile([P, H], BF16)
+        nc.vector.memset(mu_rows[:], 0.0)
+        nc.sync.dma_start(out=mu_rows[0:1, :], in_=mu.rearrange("(o h) -> o h", o=1))
+        issue_loads(RAW_BUFS)
+        internal_sb = const.tile([P, B_TILES, H], BF16)
+        nc.sync.dma_start(out=internal_sb[:], in_=internal.rearrange("(t p) h -> p t h", p=P))
+
+        ones = const.tile([P, P], BF16)
+        nc.vector.memset(ones[:], 1.0)
+        warm = const.tile([P, 1], F32)
+        nc.vector.memset(warm[:], 1.0)
+        nc.scalar.activation(out=warm[:], in_=warm[:], func=ACT.Sqrt)
+        ident = const.tile([P, P], F32)
+        make_identity(nc, ident[:])
+
+        mu_all = const.tile([P, H], BF16)
+        for half in range(2):
+            cols = slice(half * H_HALF, (half + 1) * H_HALF)
+            spread = banks.tile([P, H_HALF], F32, tag="bank")
+            nc.tensor.matmul(out=spread[:], lhsT=ones[:], rhs=mu_rows[:, cols], start=True, stop=True)
+            nc.vector.tensor_copy(out=mu_all[:, cols], in_=spread[:])
+
+        a_codes = keep.tile([P, PASSES, B], U32, align_bytes=64)
+        a_scales = keep.tile([P, PASSES, B], U8, align_bytes=64)
+        w_codes = keep.tile([P, PASSES, H], U32, align_bytes=64)
+        w_scales = keep.tile([P, PASSES, H], U8, align_bytes=64)
+
+        def transpose_slab(rows, width, local):
+            words = rows[:].bitcast(F32)
+            grouped = stage.tile([P, SLAB_ROWS * PACK], BF16, align_bytes=64, tag="grouped")
+            grouped_words = grouped[:].bitcast(F32).rearrange("p (j r u) -> p j r u", j=ROW_TILES, u=2)
+            for pair in range(ROW_TILES // 2):
+                bank = banks.tile([P, 2, 2, P], F32, tag="bank")
+                for j in range(2):
+                    for u in range(2):
+                        first = (2 * pair + j) * (width // 2) + local * PASS_WORDS + u * P
+                        nc.tensor.transpose(bank[:, j, u, :], words[:, first : first + P], ident[:])
+                nc.scalar.copy(
+                    out=grouped_words[:, 2 * pair : 2 * pair + 2, :, :],
+                    in_=bank[:].rearrange("p j u r -> p j r u"),
+                )
+            return grouped
+
+        def quantise(grouped, codes, scales):
+            nc.vector.quantize_mx(out=codes.bitcast(FP8X4), scales=scales, in_=grouped[:])
+
+        def mx_passes(acc, row_tiles, half, pass_list):
+            h_cols = slice(half * H_HALF, (half + 1) * H_HALF)
+            for t in row_tiles:
+                b_cols = slice(t * P, (t + 1) * P)
+                for c in pass_list:
+                    nc.tensor.matmul_mx(
+                        out=acc[t][:],
+                        lhsT=a_codes[:, c, b_cols].bitcast(FP8X4),
+                        lhsT_scale=a_scales[:, c, b_cols],
+                        rhs=w_codes[:, c, h_cols].bitcast(FP8X4),
+                        rhs_scale=w_scales[:, c, h_cols],
+                        start=(c == 0),
+                        stop=(c == PASSES - 1),
+                    )
+
+        all_tiles = range(B_TILES)
+        first_cols = slice(0, H_HALF)
+        second_cols = slice(H_HALF, H)
+        acc_first = [sums.tile([P, H_HALF], F32, name="acc_first%d" % t, tag="acc") for t in all_tiles]
+        result = [keep.tile([P, H], F32, name="result%d" % t) for t in all_tiles]
+        for c in range(PASSES):
+            n, local, width, last_of_chunk = where_is[c]
+            act_grouped = transpose_slab(raw[("act", n)], width, local)
+            w_grouped = transpose_slab(raw[("w", 0, n)], width, local)
+            if c > 0:
+                mx_passes(acc_first, all_tiles, 0, [c - 1])
+            quantise(act_grouped, a_codes[:, c, :], a_scales[:, c, :])
+            quantise(w_grouped, w_codes[:, c, first_cols], w_scales[:, c, first_cols])
+            if last_of_chunk:
+                issue_loads(2)
+            t = c - (PASSES - B_TILES)
+            if t >= 0:
+                nc.vector.tensor_tensor(out=result[t][:], in0=internal_sb[:, t, :], in1=mu_all[:], op=ALU.add)
+        assert len(raw) == len(loads)
+
+        steps = [list(range(c, min(c + 2, PASSES))) for c in range(0, PASSES, 2)]
+        pre_first = [keep.tile([P, H_HALF], F32, name="pre_first%d" % t) for t in all_tiles]
+        stats = [keep.tile([P, 2, 6], F32, name="stats%d" % t) for t in all_tiles]
+        acc_second = []
+        for s, step in enumerate(steps):
+            grouped_list = []
+            for c in step:
+                n, local, width, last_of_chunk = where_is[c]
+                grouped_list.append(transpose_slab(raw[("w", 1, n)], width, local))
+            if s == 0:
+                mx_passes(acc_first, all_tiles, 0, [PASSES - 1])
+                for t in all_tiles:
+                    nc.vector.tensor_copy(out=pre_first[t][:], in_=acc_first[t][:])
+                for t in all_tiles:
+                    acc_second.append(sums.tile([P, H_HALF], F32, name="acc_second%d" % t, tag="acc"))
+            else:
+                mx_passes(acc_second, (0, 1), 1, steps[s - 1])
+            for c, grouped in zip(step, grouped_list):
+                quantise(grouped, w_codes[:, c, second_cols], w_scales[:, c, second_cols])
+            if s < B_TILES:
+                nc.vector.bn_stats(out=stats[s][:, 0, :], in_=pre_first[s][:])
+        mx_passes(acc_second, (0, 1), 1, steps[-1])
+        mx_passes(acc_second, (2,), 1, range(PASSES))
+        mx_passes(acc_second, (3,), 1, range(PASSES))
+
+        for t in all_tiles:
+            nc.vector.bn_stats(out=stats[t][:, 1, :], in_=acc_second[t][:])
+            mean_var = keep.tile([P, 2], F32, name="mean_var%d" % t)
+            nc.vector.bn_aggr(out=mean_var[:], in_=stats[t][:].rearrange("p a s -> p (a s)"))
+            sd = keep.tile([P, 1], F32, name="sd%d" % t)
+            nc.scalar.activation(out=sd[:], in_=mean_var[:, 1:2], func=ACT.Sqrt)
+            nc.vector.tensor_scalar_add(out=sd[:], in0=sd[:], scalar1=EPS)
+            rstd = keep.tile([P, 1], F32, name="rstd%d" % t)
+            nc.vector.reciprocal(out=rstd[:], in_=sd[:])
+            shift = keep.tile([P, 1], F32, name="shift%d" % t)
+            nc.vector.tensor_scalar(
+                out=shift[:], in0=mean_var[:, 0:1], scalar1=rstd[:, 0:1], scalar2=-1.0, op0=ALU.mult, op1=ALU.mult
+            )
+            for cols, pre in ((first_cols, pre_first[t]), (second_cols, acc_second[t])):
+                nc.vector.scalar_tensor_tensor(
+                    out=result[t][:, cols],
+                    in0=pre[:],
+                    scalar=rstd[:, 0:1],
+                    in1=result[t][:, cols],
+                    op0=ALU.mult,
+                    op1=ALU.add,
+                )
+                nc.scalar.activation(
+                    out=result[t][:, cols], in_=result[t][:, cols], func=ACT.Relu, bias=shift[:, 0:1], scale=1.0
+                )
+                nc.sync.dma_start(out=out[t * P : (t + 1) * P, cols], in_=result[t][:, cols])

@@ -102,7 +102,8 @@ def tile_sparsegatedrnncell_pb_kernel(tc, x, hx, sy, internal, W_ih, W_hh, W_sh,
                     for u in range(2):
                         first = (2 * pair + j) * (width // 2) + local * PASS_WORDS + u * P
                         nc.tensor.transpose(bank[:, j, u, :], words[:, first : first + P], ident[:])
-                nc.scalar.copy(
+                copy_out = (nc.scalar.copy, nc.vector.tensor_copy)[pair]
+                copy_out(
                     out=grouped_words[:, 2 * pair : 2 * pair + 2, :, :],
                     in_=bank[:].rearrange("p j u r -> p j r u"),
                 )

@@ -24,6 +24,7 @@ K_TOTAL = 512 + 1024 + 4096
 PASSES = K_TOTAL // K_PASS
 K_CHUNK = 2 * K_PASS
 RAW_BUFS = 8
+LAG = 3
 EPS = 0.0001
 
 FLOPS = 2 * B * H * K_TOTAL
@@ -102,8 +103,7 @@ def tile_sparsegatedrnncell_pb_kernel(tc, x, hx, sy, internal, W_ih, W_hh, W_sh,
                     for u in range(2):
                         first = (2 * pair + j) * (width // 2) + local * PASS_WORDS + u * P
                         nc.tensor.transpose(bank[:, j, u, :], words[:, first : first + P], ident[:])
-                copy_out = (nc.scalar.copy, nc.vector.tensor_copy)[pair]
-                copy_out(
+                nc.scalar.copy(
                     out=grouped_words[:, 2 * pair : 2 * pair + 2, :, :],
                     in_=bank[:].rearrange("p j u r -> p j r u"),
                 )
@@ -130,47 +130,52 @@ def tile_sparsegatedrnncell_pb_kernel(tc, x, hx, sy, internal, W_ih, W_hh, W_sh,
         all_tiles = range(B_TILES)
         first_cols = slice(0, H_HALF)
         second_cols = slice(H_HALF, H)
-        acc_first = [sums.tile([P, H_HALF], F32, name="acc_first%d" % t, tag="acc") for t in all_tiles]
-        result = [keep.tile([P, H], F32, name="result%d" % t) for t in all_tiles]
+        slabs = []
+        runs = []
         for c in range(PASSES):
-            n, local, width, last_of_chunk = where_is[c]
-            act_grouped = transpose_slab(raw[("act", n)], width, local)
-            w_grouped = transpose_slab(raw[("w", 0, n)], width, local)
-            if c > 0:
-                mx_passes(acc_first, all_tiles, 0, [c - 1])
-            quantise(act_grouped, a_codes[:, c, :], a_scales[:, c, :])
-            quantise(w_grouped, w_codes[:, c, first_cols], w_scales[:, c, first_cols])
-            if last_of_chunk:
-                issue_loads(2)
-            t = c - (PASSES - B_TILES)
-            if t >= 0:
-                nc.vector.tensor_tensor(out=result[t][:], in0=internal_sb[:, t, :], in1=mu_all[:], op=ALU.add)
-        assert len(raw) == len(loads)
+            n = where_is[c][0]
+            slabs.append((("act", n), c, a_codes[:, c, :], a_scales[:, c, :]))
+            slabs.append((("w", 0, n), c, w_codes[:, c, first_cols], w_scales[:, c, first_cols]))
+            runs.append((0, c, (0, 1)))
+            runs.append((0, c, (2, 3)))
+        part1_slabs = len(slabs)
+        for c in range(PASSES):
+            n = where_is[c][0]
+            slabs.append((("w", 1, n), c, w_codes[:, c, second_cols], w_scales[:, c, second_cols]))
+            runs.append((1, c, (0, 1)))
 
-        steps = [list(range(c, min(c + 2, PASSES))) for c in range(0, PASSES, 2)]
+        acc = {0: [sums.tile([P, H_HALF], F32, name="acc_first%d" % t, tag="acc") for t in all_tiles], 1: []}
+        result = [keep.tile([P, H], F32, name="result%d" % t) for t in all_tiles]
         pre_first = [keep.tile([P, H_HALF], F32, name="pre_first%d" % t) for t in all_tiles]
         stats = [keep.tile([P, 2, 6], F32, name="stats%d" % t) for t in all_tiles]
-        acc_second = []
-        for s, step in enumerate(steps):
-            grouped_list = []
-            for c in step:
+        for i in range(len(slabs) + LAG):
+            if i < len(slabs):
+                key, c, codes, scales = slabs[i]
                 n, local, width, last_of_chunk = where_is[c]
-                grouped_list.append(transpose_slab(raw[("w", 1, n)], width, local))
-            if s == 0:
-                mx_passes(acc_first, all_tiles, 0, [PASSES - 1])
-                for t in all_tiles:
-                    nc.vector.tensor_copy(out=pre_first[t][:], in_=acc_first[t][:])
-                for t in all_tiles:
-                    acc_second.append(sums.tile([P, H_HALF], F32, name="acc_second%d" % t, tag="acc"))
-            else:
-                mx_passes(acc_second, (0, 1), 1, steps[s - 1])
-            for c, grouped in zip(step, grouped_list):
-                quantise(grouped, w_codes[:, c, second_cols], w_scales[:, c, second_cols])
-            if s < B_TILES:
-                nc.vector.bn_stats(out=stats[s][:, 0, :], in_=pre_first[s][:])
-        mx_passes(acc_second, (0, 1), 1, steps[-1])
-        mx_passes(acc_second, (2,), 1, range(PASSES))
-        mx_passes(acc_second, (3,), 1, range(PASSES))
+                grouped = transpose_slab(raw[key], width, local)
+                if last_of_chunk and len(raw) < len(loads):
+                    issue_loads(1)
+            if i >= LAG:
+                half, c_run, row_tiles = runs[i - LAG]
+                mx_passes(acc[half], row_tiles, half, [c_run])
+                if half == 0 and c_run == PASSES - 1:
+                    for t in row_tiles:
+                        nc.vector.tensor_copy(out=pre_first[t][:], in_=acc[0][t][:])
+                        acc[1].append(sums.tile([P, H_HALF], F32, name="acc_second%d" % t, tag="acc"))
+            if i < len(slabs):
+                quantise(grouped, codes, scales)
+            if i < part1_slabs and i % 2 == 1:
+                t = i // 2 - (PASSES - B_TILES)
+                if t >= 0:
+                    nc.vector.tensor_tensor(out=result[t][:], in0=internal_sb[:, t, :], in1=mu_all[:], op=ALU.add)
+            if i >= part1_slabs:
+                t = i - part1_slabs - (LAG + 1)
+                if 0 <= t < B_TILES:
+                    nc.vector.bn_stats(out=stats[t][:, 0, :], in_=pre_first[t][:])
+        assert len(raw) == len(loads)
+        acc_second = acc[1]
+        for t in (2, 3):
+            mx_passes(acc_second, (t,), 1, range(PASSES))
 
         for t in all_tiles:
             nc.vector.bn_stats(out=stats[t][:, 1, :], in_=acc_second[t][:])

@@ -24,7 +24,8 @@ K_TOTAL = 512 + 1024 + 4096
 PASSES = K_TOTAL // K_PASS
 K_CHUNK = 2 * K_PASS
 RAW_BUFS = 8
-LAG = 3
+GROUP = 2
+LAG = 2
 EPS = 0.0001
 
 FLOPS = 2 * B * H * K_TOTAL
@@ -148,30 +149,38 @@ def tile_sparsegatedrnncell_pb_kernel(tc, x, hx, sy, internal, W_ih, W_hh, W_sh,
         result = [keep.tile([P, H], F32, name="result%d" % t) for t in all_tiles]
         pre_first = [keep.tile([P, H_HALF], F32, name="pre_first%d" % t) for t in all_tiles]
         stats = [keep.tile([P, 2, 6], F32, name="stats%d" % t) for t in all_tiles]
-        for i in range(len(slabs) + LAG):
-            if i < len(slabs):
-                key, c, codes, scales = slabs[i]
-                n, local, width, last_of_chunk = where_is[c]
-                grouped = transpose_slab(raw[key], width, local)
-                if last_of_chunk and len(raw) < len(loads):
-                    issue_loads(1)
-            if i >= LAG:
-                half, c_run, row_tiles = runs[i - LAG]
-                mx_passes(acc[half], row_tiles, half, [c_run])
-                if half == 0 and c_run == PASSES - 1:
-                    for t in row_tiles:
-                        nc.vector.tensor_copy(out=pre_first[t][:], in_=acc[0][t][:])
-                        acc[1].append(sums.tile([P, H_HALF], F32, name="acc_second%d" % t, tag="acc"))
-            if i < len(slabs):
-                quantise(grouped, codes, scales)
-            if i < part1_slabs and i % 2 == 1:
-                t = i // 2 - (PASSES - B_TILES)
-                if t >= 0:
-                    nc.vector.tensor_tensor(out=result[t][:], in0=internal_sb[:, t, :], in1=mu_all[:], op=ALU.add)
-            if i >= part1_slabs:
-                t = i - part1_slabs - (LAG + 1)
-                if 0 <= t < B_TILES:
-                    nc.vector.bn_stats(out=stats[t][:, 0, :], in_=pre_first[t][:])
+        groups = [range(g, min(g + GROUP, len(slabs))) for g in range(0, len(slabs), GROUP)]
+        grouped = {}
+        for g in range(len(groups) + LAG):
+            if g < len(groups):
+                for i in groups[g]:
+                    key, c, codes, scales = slabs[i]
+                    n, local, width, last_of_chunk = where_is[c]
+                    grouped[i] = transpose_slab(raw[key], width, local)
+                    if last_of_chunk and len(raw) < len(loads):
+                        issue_loads(1)
+            if g >= LAG:
+                for r in groups[g - LAG]:
+                    half, c_run, row_tiles = runs[r]
+                    mx_passes(acc[half], row_tiles, half, [c_run])
+                    if half == 0 and c_run == PASSES - 1:
+                        for t in row_tiles:
+                            nc.vector.tensor_copy(out=pre_first[t][:], in_=acc[0][t][:])
+                            acc[1].append(sums.tile([P, H_HALF], F32, name="acc_second%d" % t, tag="acc"))
+            if g < len(groups):
+                for i in groups[g]:
+                    key, c, codes, scales = slabs[i]
+                    quantise(grouped[i], codes, scales)
+                    if i < part1_slabs and i % 2 == 1:
+                        t = i // 2 - (PASSES - B_TILES)
+                        if t >= 0:
+                            nc.vector.tensor_tensor(
+                                out=result[t][:], in0=internal_sb[:, t, :], in1=mu_all[:], op=ALU.add
+                            )
+                    if i >= part1_slabs:
+                        t = i - part1_slabs - GROUP * LAG
+                        if 0 <= t < B_TILES:
+                            nc.vector.bn_stats(out=stats[t][:, 0, :], in_=pre_first[t][:])
         assert len(raw) == len(loads)
         acc_second = acc[1]
         for t in (2, 3):

@@ -24,8 +24,8 @@ K_TOTAL = 512 + 1024 + 4096
 PASSES = K_TOTAL // K_PASS
 K_CHUNK = 2 * K_PASS
 RAW_BUFS = 8
-GROUP = 2
-LAG = 2
+GROUP = 1
+LAG = 3
 EPS = 0.0001
 
 FLOPS = 2 * B * H * K_TOTAL
@@ -94,7 +94,7 @@ def tile_sparsegatedrnncell_pb_kernel(tc, x, hx, sy, internal, W_ih, W_hh, W_sh,
         w_codes = keep.tile([P, PASSES, H], U32, align_bytes=64)
         w_scales = keep.tile([P, PASSES, H], U8, align_bytes=64)
 
-        def transpose_slab(rows, width, local):
+        def transpose_slab(rows, width, local, second_copy):
             words = rows[:].bitcast(F32)
             grouped = stage.tile([P, SLAB_ROWS * PACK], BF16, align_bytes=64, tag="grouped")
             grouped_words = grouped[:].bitcast(F32).rearrange("p (j r u) -> p j r u", j=ROW_TILES, u=2)
@@ -104,7 +104,8 @@ def tile_sparsegatedrnncell_pb_kernel(tc, x, hx, sy, internal, W_ih, W_hh, W_sh,
                     for u in range(2):
                         first = (2 * pair + j) * (width // 2) + local * PASS_WORDS + u * P
                         nc.tensor.transpose(bank[:, j, u, :], words[:, first : first + P], ident[:])
-                nc.scalar.copy(
+                copy_out = (nc.scalar.copy, second_copy)[pair]
+                copy_out(
                     out=grouped_words[:, 2 * pair : 2 * pair + 2, :, :],
                     in_=bank[:].rearrange("p j u r -> p j r u"),
                 )
@@ -156,7 +157,8 @@ def tile_sparsegatedrnncell_pb_kernel(tc, x, hx, sy, internal, W_ih, W_hh, W_sh,
                 for i in groups[g]:
                     key, c, codes, scales = slabs[i]
                     n, local, width, last_of_chunk = where_is[c]
-                    grouped[i] = transpose_slab(raw[key], width, local)
+                    second_copy = nc.vector.tensor_copy if i % 2 == 0 else nc.scalar.copy
+                    grouped[i] = transpose_slab(raw[key], width, local, second_copy)
                     if last_of_chunk and len(raw) < len(loads):
                         issue_loads(1)
             if g >= LAG:

from contextlib import ExitStack

import concourse.mybir as mybir
from concourse.masks import make_identity

F32 = mybir.dt.float32
BF16 = mybir.dt.bfloat16
U32 = mybir.dt.uint32
U8 = mybir.dt.uint8
FP8X4 = mybir.dt.float8_e4m3fn_x4
ALU = mybir.AluOpType
ACT = mybir.ActivationFunctionType

P = 128
PACK = 4
K_PASS = P * PACK
PASS_WORDS = K_PASS // 2
B, H = 512, 1024
B_TILES = B // P
H_HALF = 512
SLAB_ROWS = 512
ROW_TILES = SLAB_ROWS // P
K_TOTAL = 512 + 1024 + 4096
PASSES = K_TOTAL // K_PASS
K_CHUNK = 2 * K_PASS
RAW_BUFS = 8
GROUP = 1
LAG = 3
EPS = 0.0001

FLOPS = 2 * B * H * K_TOTAL


def tile_sparsegatedrnncell_pb_kernel(tc, x, hx, sy, internal, W_ih, W_hh, W_sh, mu, out):
    nc = tc.nc
    with ExitStack() as ctx:
        const = ctx.enter_context(tc.tile_pool(name="const", bufs=1))
        keep = ctx.enter_context(tc.tile_pool(name="keep", bufs=1))
        raw_pool = ctx.enter_context(tc.tile_pool(name="raw_pool", bufs=RAW_BUFS))
        stage = ctx.enter_context(tc.tile_pool(name="stage", bufs=4))
        banks = ctx.enter_context(tc.psum_pool(name="banks", bufs=4))
        sums = ctx.enter_context(tc.psum_pool(name="sums", bufs=4))
        ctx.enter_context(tc.manual_schedule())

        chunks = []
        where_is = []
        for act, weight in ((x, W_ih), (hx, W_hh), (sy, W_sh)):
            for k0 in range(0, act.shape[1], K_CHUNK):
                width = min(K_CHUNK, act.shape[1] - k0)
                for local in range(width // K_PASS):
                    where_is.append((len(chunks), local, width, local == width // K_PASS - 1))
                chunks.append((act, weight, k0, width))
        loads = []
        for n, (act, weight, k0, width) in enumerate(chunks):
            loads.append((("act", n), act, 0, k0, width))
            loads.append((("w", 0, n), weight, 0, k0, width))
        for n, (act, weight, k0, width) in enumerate(chunks):
            loads.append((("w", 1, n), weight, H_HALF, k0, width))
        raw = {}

        def issue_loads(count):
            for key, source, row0, k0, width in loads[len(raw) : len(raw) + count]:
                rows = raw_pool.tile([P, ROW_TILES * K_CHUNK], BF16, name="rows", tag="rows")
                nc.sync.dma_start(
                    out=rows[:, 0 : ROW_TILES * width].rearrange("p (j k) -> p j k", j=ROW_TILES),
                    in_=source[row0 : row0 + SLAB_ROWS, k0 : k0 + width].rearrange("(j p) k -> p j k", p=P),
                )
                raw[key] = rows

        mu_rows = const.tile([P, H], BF16)
        nc.vector.memset(mu_rows[:], 0.0)
        nc.sync.dma_start(out=mu_rows[0:1, :], in_=mu.rearrange("(o h) -> o h", o=1))
        issue_loads(RAW_BUFS)
        internal_sb = const.tile([P, B_TILES, H], BF16)
        nc.sync.dma_start(out=internal_sb[:], in_=internal.rearrange("(t p) h -> p t h", p=P))

        ones = const.tile([P, P], BF16)
        nc.vector.memset(ones[:], 1.0)
        warm = const.tile([P, 1], F32)
        nc.vector.memset(warm[:], 1.0)
        nc.scalar.activation(out=warm[:], in_=warm[:], func=ACT.Sqrt)
        ident = const.tile([P, P], F32)
        make_identity(nc, ident[:])

        mu_all = const.tile([P, H], BF16)
        for half in range(2):
            cols = slice(half * H_HALF, (half + 1) * H_HALF)
            spread = banks.tile([P, H_HALF], F32, tag="bank")
            nc.tensor.matmul(out=spread[:], lhsT=ones[:], rhs=mu_rows[:, cols], start=True, stop=True)
            nc.vector.tensor_copy(out=mu_all[:, cols], in_=spread[:])

        a_codes = keep.tile([P, PASSES, B], U32, align_bytes=64)
        a_scales = keep.tile([P, PASSES, B], U8, align_bytes=64)
        w_codes = keep.tile([P, PASSES, H], U32, align_bytes=64)
        w_scales = keep.tile([P, PASSES, H], U8, align_bytes=64)

        def transpose_slab(rows, width, local, second_copy):
            words = rows[:].bitcast(F32)
            grouped = stage.tile([P, SLAB_ROWS * PACK], BF16, align_bytes=64, tag="grouped")
            grouped_words = grouped[:].bitcast(F32).rearrange("p (j r u) -> p j r u", j=ROW_TILES, u=2)
            for pair in range(ROW_TILES // 2):
                bank = banks.tile([P, 2, 2, P], F32, tag="bank")
                for j in range(2):
                    for u in range(2):
                        first = (2 * pair + j) * (width // 2) + local * PASS_WORDS + u * P
                        nc.tensor.transpose(bank[:, j, u, :], words[:, first : first + P], ident[:])
                copy_out = (nc.scalar.copy, second_copy)[pair]
                copy_out(
                    out=grouped_words[:, 2 * pair : 2 * pair + 2, :, :],
                    in_=bank[:].rearrange("p j u r -> p j r u"),
                )
            return grouped

        def quantise(grouped, codes, scales):
            nc.vector.quantize_mx(out=codes.bitcast(FP8X4), scales=scales, in_=grouped[:])

        def mx_passes(acc, row_tiles, half, pass_list):
            h_cols = slice(half * H_HALF, (half + 1) * H_HALF)
            for t in row_tiles:
                b_cols = slice(t * P, (t + 1) * P)
                for c in pass_list:
                    nc.tensor.matmul_mx(
                        out=acc[t][:],
                        lhsT=a_codes[:, c, b_cols].bitcast(FP8X4),
                        lhsT_scale=a_scales[:, c, b_cols],
                        rhs=w_codes[:, c, h_cols].bitcast(FP8X4),
                        rhs_scale=w_scales[:, c, h_cols],
                        start=(c == 0),
                        stop=(c == PASSES - 1),
                    )

        all_tiles = range(B_TILES)
        first_cols = slice(0, H_HALF)
        second_cols = slice(H_HALF, H)
        slabs = []
        runs = []
        for c in range(PASSES):
            n = where_is[c][0]
            slabs.append((("act", n), c, a_codes[:, c, :], a_scales[:, c, :]))
            slabs.append((("w", 0, n), c, w_codes[:, c, first_cols], w_scales[:, c, first_cols]))
            runs.append((0, c, (0, 1)))
            runs.append((0, c, (2, 3)))
        part1_slabs = len(slabs)
        for c in range(PASSES):
            n = where_is[c][0]
            slabs.append((("w", 1, n), c, w_codes[:, c, second_cols], w_scales[:, c, second_cols]))
            runs.append((1, c, (0, 1)))

        acc = {0: [sums.tile([P, H_HALF], F32, name="acc_first%d" % t, tag="acc") for t in all_tiles], 1: []}
        result = [keep.tile([P, H], F32, name="result%d" % t) for t in all_tiles]
        pre_first = [keep.tile([P, H_HALF], F32, name="pre_first%d" % t) for t in all_tiles]
        stats = [keep.tile([P, 2, 6], F32, name="stats%d" % t) for t in all_tiles]
        groups = [range(g, min(g + GROUP, len(slabs))) for g in range(0, len(slabs), GROUP)]
        grouped = {}
        for g in range(len(groups) + LAG):
            if g < len(groups):
                for i in groups[g]:
                    key, c, codes, scales = slabs[i]
                    n, local, width, last_of_chunk = where_is[c]
                    second_copy = nc.vector.tensor_copy if i % 2 == 0 else nc.scalar.copy
                    grouped[i] = transpose_slab(raw[key], width, local, second_copy)
                    if last_of_chunk and len(raw) < len(loads):
                        issue_loads(1)
            if g >= LAG:
                for r in groups[g - LAG]:
                    half, c_run, row_tiles = runs[r]
                    mx_passes(acc[half], row_tiles, half, [c_run])
                    if half == 0 and c_run == PASSES - 1:
                        for t in row_tiles:
                            nc.vector.tensor_copy(out=pre_first[t][:], in_=acc[0][t][:])
                            acc[1].append(sums.tile([P, H_HALF], F32, name="acc_second%d" % t, tag="acc"))
            if g < len(groups):
                for i in groups[g]:
                    key, c, codes, scales = slabs[i]
                    quantise(grouped[i], codes, scales)
                    if i < part1_slabs and i % 2 == 1:
                        t = i // 2 - (PASSES - B_TILES)
                        if t >= 0:
                            nc.vector.tensor_tensor(
                                out=result[t][:], in0=internal_sb[:, t, :], in1=mu_all[:], op=ALU.add
                            )
                    if i >= part1_slabs:
                        t = i - part1_slabs - GROUP * LAG
                        if 0 <= t < B_TILES:
                            nc.vector.bn_stats(out=stats[t][:, 0, :], in_=pre_first[t][:])
        assert len(raw) == len(loads)
        acc_second = acc[1]
        for t in (2, 3):
            mx_passes(acc_second, (t,), 1, range(PASSES))

        for t in all_tiles:
            nc.vector.bn_stats(out=stats[t][:, 1, :], in_=acc_second[t][:])
            mean_var = keep.tile([P, 2], F32, name="mean_var%d" % t)
            nc.vector.bn_aggr(out=mean_var[:], in_=stats[t][:].rearrange("p a s -> p (a s)"))
            sd = keep.tile([P, 1], F32, name="sd%d" % t)
            nc.scalar.activation(out=sd[:], in_=mean_var[:, 1:2], func=ACT.Sqrt)
            nc.vector.tensor_scalar_add(out=sd[:], in0=sd[:], scalar1=EPS)
            rstd = keep.tile([P, 1], F32, name="rstd%d" % t)
            nc.vector.reciprocal(out=rstd[:], in_=sd[:])
            shift = keep.tile([P, 1], F32, name="shift%d" % t)
            nc.vector.tensor_scalar(
                out=shift[:], in0=mean_var[:, 0:1], scalar1=rstd[:, 0:1], scalar2=-1.0, op0=ALU.mult, op1=ALU.mult
            )
            for cols, pre in ((first_cols, pre_first[t]), (second_cols, acc_second[t])):
                nc.vector.scalar_tensor_tensor(
                    out=result[t][:, cols],
                    in0=pre[:],
                    scalar=rstd[:, 0:1],
                    in1=result[t][:, cols],
                    op0=ALU.mult,
                    op1=ALU.add,
                )
                nc.scalar.activation(
                    out=result[t][:, cols], in_=result[t][:, cols], func=ACT.Relu, bias=shift[:, 0:1], scale=1.0
                )
                nc.sync.dma_start(out=out[t * P : (t + 1) * P, cols], in_=result[t][:, cols])
